import numpy as np
import ml_dtypes

BF16 = ml_dtypes.bfloat16


def bf(x):
    return np.asarray(x, np.float32).astype(BF16)


def f32(x):
    return np.asarray(x, np.float32)


def f64(x):
    return np.asarray(x).astype(np.float64)


def striped(idx):
    return np.tile(idx.reshape(-1, 16).T, (8, 1))


C, S, N, B, P = 128, 512, 256, 2, 128
SLOPE = 0.01
KEEP = 0.75
SHARP = 2.0


def setup_inputs():
    return {"base": f32(np.random.standard_normal((C, S))), "x": f32(np.random.standard_normal((C, N))), "score": f32(SHARP * np.random.standard_normal((B, P, P))), "mask": f32(np.random.random((B, P, P)) < KEEP), "w": f32(np.random.standard_normal((C, C)) / np.sqrt(C)), "b": f32(0.1 * np.random.standard_normal((C, 1))), "offs": striped(np.random.permutation(S)[:N])}


def reference(base, x, score, mask, w, b, offs):
    idx = offs[:16].T.reshape(-1)
    e = np.exp(f64(score))
    att = e / e.sum(axis=2, keepdims=True) * f64(mask)
    agg = np.einsum("tik,dtk->dti", att, f64(x).reshape(C, B, P)).reshape(C, N)
    v = f64(x) + f64(w).T @ agg + f64(b)
    slope = np.where(v >= 0.0, 1.0, SLOPE)
    out = f64(base).copy()
    out[:, idx] = v * slope
    return out

@@ -1,0 +1,81 @@
+import concourse.mybir as mybir
+from concourse.masks import make_identity
+
+F32, BF16, U16 = mybir.dt.float32, mybir.dt.bfloat16, mybir.dt.uint16
+ALU = mybir.AluOpType
+ACT = mybir.ActivationFunctionType
+AXIS = mybir.AxisListType
+
+C, S, N, B, P = 128, 512, 256, 2, 128
+SLOPE = 0.01
+FLOPS = 2 * C * C * N + 2 * C * P * N
+
+
+def tile_multiheadgraphconvlayer_kernel(tc, base, x, score, mask, w, b, offs, out):
+    nc = tc.nc
+    with tc.tile_pool(name="held", bufs=1) as held, tc.psum_pool(name="banks", bufs=1) as banks:
+        score_sb = held.tile([P, B, P], F32, name="score_sb")
+        nc.sync.dma_start(score_sb[:], score.rearrange("t i k -> i t k"))
+        mask_sb = held.tile([P, B, P], F32, name="mask_sb")
+        nc.scalar.dma_start(mask_sb[:], mask.rearrange("t i k -> i t k"))
+        x_sb = held.tile([C, N], F32, name="x_sb")
+        nc.sync.dma_start(x_sb[:], x)
+        w_sb = held.tile([C, C], F32, name="w_sb")
+        nc.scalar.dma_start(w_sb[:], w)
+        b_sb = held.tile([C, 1], F32, name="b_sb")
+        nc.sync.dma_start(b_sb[:], b)
+        offsets = held.tile([128, N // 16], U16, name="offsets")
+        nc.sync.dma_start(offsets[:], offs)
+        window = held.tile([C, S], F32, name="window")
+        nc.sync.dma_start(window[:], base)
+
+        scratch = held.tile([P, 1], F32, name="scratch")
+        nc.vector.memset(scratch[:], 0.0)
+        nc.scalar.activation(scratch[:], scratch[:], ACT.Exp)
+
+        identity = held.tile([P, P], BF16, name="identity")
+        make_identity(nc, identity[:])
+
+        negmax = held.tile([P, B], F32, name="negmax")
+        e = held.tile([P, B, P], F32, name="e")
+        rowsum = held.tile([P, B], F32, name="rowsum")
+        rinv = held.tile([P, B], F32, name="rinv")
+        for t in range(B):
+            nc.vector.tensor_reduce(negmax[:, t : t + 1], score_sb[:, t, :], axis=AXIS.X, op=ALU.max, negate=True)
+            nc.scalar.activation(
+                e[:, t, :], score_sb[:, t, :], ACT.Exp, bias=negmax[:, t : t + 1], accum_out=rowsum[:, t : t + 1]
+            )
+        x_bf = held.tile([C, N], BF16, name="x_bf")
+        nc.vector.tensor_copy(x_bf[:], x_sb[:])
+        w_bf = held.tile([C, C], BF16, name="w_bf")
+        nc.vector.tensor_copy(w_bf[:], w_sb[:])
+        yT_ps = [banks.tile([P, C], F32, name=f"yT_ps{t}") for t in range(B)]
+        yT = held.tile([P, B, C], BF16, name="yT")
+        for t in range(B):
+            nc.tensor.matmul(yT_ps[t][:], lhsT=x_bf[:, t * P : (t + 1) * P], rhs=w_bf[:], start=True, stop=True)
+            nc.scalar.copy(yT[:, t, :], yT_ps[t][:])
+
+        att = held.tile([P, B, P], BF16, name="att")
+        attT_ps = [banks.tile([P, P], BF16, name=f"attT_ps{t}") for t in range(B)]
+        for t in range(B):
+            nc.vector.reciprocal(rinv[:, t : t + 1], rowsum[:, t : t + 1])
+            nc.vector.scalar_tensor_tensor(
+                att[:, t, :], e[:, t, :], rinv[:, t : t + 1], mask_sb[:, t, :], ALU.mult, ALU.mult
+            )
+            nc.tensor.transpose(attT_ps[t][:], att[:, t, :], identity[:])
+
+        attT = held.tile([P, B, P], BF16, name="attT")
+        v_ps = [banks.tile([C, P], F32, name=f"v_ps{t}") for t in range(B)]
+        for t in range(B):
+            nc.vector.tensor_copy(attT[:, t, :], attT_ps[t][:])
+            nc.tensor.matmul(v_ps[t][:], lhsT=yT[:, t, :], rhs=attT[:, t, :], start=True, stop=True)
+
+        v = held.tile([C, N], F32, name="v")
+        slope = held.tile([C, N], F32, name="slope")
+        for t in range(B):
+            cols = slice(t * P, (t + 1) * P)
+            nc.vector.scalar_tensor_tensor(v[:, cols], v_ps[t][:], b_sb[:, 0:1], x_sb[:, cols], ALU.add, ALU.add)
+            nc.vector.tensor_scalar(slope[:, cols], v[:, cols], 0.0, SLOPE, ALU.is_ge, ALU.max)
+
+        nc.vector.tensor_tensor(window[:].indirect(offsets[:]), v[:], slope[:], ALU.mult)
+        nc.sync.dma_start(out, window[:])

@@ -49,6 +49,13 @@ def tile_multiheadgraphconvlayer_kernel(tc, base, x, score, mask, w, b, offs, ou
         nc.vector.tensor_copy(x_bf[:], x_sb[:])
         w_bf = held.tile([C, C], BF16, name="w_bf")
         nc.vector.tensor_copy(w_bf[:], w_sb[:])
+        x1 = x_sb[:, P:N]
+        x1_high = x1.bitcast(BF16)[:, 1 : 2 * P : 2]
+        rest = held.tile([C, P], F32, name="rest")
+        nc.gpsimd.tensor_tensor(rest[:], x1, x1_high, ALU.subtract)
+        rest_high = rest[:].bitcast(BF16)[:, 1 : 2 * P : 2]
+        x1_low = held.tile([C, P], BF16, name="x1_low")
+        nc.gpsimd.tensor_tensor(x1_low[:], rest[:], rest_high, ALU.subtract)
         yT_ps = [banks.tile([P, C], F32, name=f"yT_ps{t}") for t in range(B)]
         yT = held.tile([P, B, C], BF16, name="yT")
         for t in range(B):
@@ -66,16 +73,20 @@ def tile_multiheadgraphconvlayer_kernel(tc, base, x, score, mask, w, b, offs, ou
 
         attT = held.tile([P, B, P], BF16, name="attT")
         v_ps = [banks.tile([C, P], F32, name=f"v_ps{t}") for t in range(B)]
+        for n, term in enumerate((x1_high, rest_high, x1_low[:])):
+            nc.tensor.matmul(v_ps[1][:], lhsT=identity[:], rhs=term, start=n == 0, stop=False)
         for t in range(B):
             nc.vector.tensor_copy(attT[:, t, :], attT_ps[t][:])
-            nc.tensor.matmul(v_ps[t][:], lhsT=yT[:, t, :], rhs=attT[:, t, :], start=True, stop=True)
+            nc.tensor.matmul(v_ps[t][:], lhsT=yT[:, t, :], rhs=attT[:, t, :], start=t == 0, stop=True)
 
+        negb = held.tile([C, 1], F32, name="negb")
+        nc.scalar.mul(negb[:], b_sb[:], -1.0)
         v = held.tile([C, N], F32, name="v")
         slope = held.tile([C, N], F32, name="slope")
-        for t in range(B):
-            cols = slice(t * P, (t + 1) * P)
-            nc.vector.scalar_tensor_tensor(v[:, cols], v_ps[t][:], b_sb[:, 0:1], x_sb[:, cols], ALU.add, ALU.add)
-            nc.vector.tensor_scalar(slope[:, cols], v[:, cols], 0.0, SLOPE, ALU.is_ge, ALU.max)
+        nc.vector.scalar_tensor_tensor(v[:, 0:P], v_ps[0][:], b_sb[:, 0:1], x_sb[:, 0:P], ALU.add, ALU.add)
+        nc.vector.tensor_scalar(slope[:, P:N], v_ps[1][:], negb[:, 0:1], SLOPE, ALU.is_ge, ALU.max)
+        nc.vector.tensor_scalar(v[:, P:N], v_ps[1][:], b_sb[:, 0:1], None, ALU.add)
+        nc.vector.tensor_scalar(slope[:, 0:P], v[:, 0:P], 0.0, SLOPE, ALU.is_ge, ALU.max)
 
         nc.vector.tensor_tensor(window[:].indirect(offsets[:]), v[:], slope[:], ALU.mult)
         nc.sync.dma_start(out, window[:])

@@ -48,7 +48,7 @@ def tile_multiheadgraphconvlayer_kernel(tc, base, x, score, mask, w, b, offs, ou
         x_bf = held.tile([C, N], BF16, name="x_bf")
         nc.vector.tensor_copy(x_bf[:], x_sb[:])
         w_bf = held.tile([C, C], BF16, name="w_bf")
-        nc.vector.tensor_copy(w_bf[:], w_sb[:])
+        nc.scalar.copy(w_bf[:], w_sb[:])
         x1 = x_sb[:, P:N]
         x1_high = x1.bitcast(BF16)[:, 1 : 2 * P : 2]
         rest = held.tile([C, P], F32, name="rest")

@@ -16,10 +16,10 @@ def tile_multiheadgraphconvlayer_kernel(tc, base, x, score, mask, w, b, offs, ou
     with tc.tile_pool(name="held", bufs=1) as held, tc.psum_pool(name="banks", bufs=1) as banks:
         score_sb = held.tile([P, B, P], F32, name="score_sb")
         nc.sync.dma_start(score_sb[:], score.rearrange("t i k -> i t k"))
-        mask_sb = held.tile([P, B, P], F32, name="mask_sb")
-        nc.scalar.dma_start(mask_sb[:], mask.rearrange("t i k -> i t k"))
         x_sb = held.tile([C, N], F32, name="x_sb")
-        nc.sync.dma_start(x_sb[:], x)
+        nc.scalar.dma_start(x_sb[:], x)
+        mask_sb = held.tile([P, B, P], F32, name="mask_sb")
+        nc.sync.dma_start(mask_sb[:], mask.rearrange("t i k -> i t k"))
         w_sb = held.tile([C, C], F32, name="w_sb")
         nc.scalar.dma_start(w_sb[:], w)
         b_sb = held.tile([C, 1], F32, name="b_sb")

@@ -56,7 +56,7 @@ def tile_multiheadgraphconvlayer_kernel(tc, base, x, score, mask, w, b, offs, ou
         rest_high = rest[:].bitcast(BF16)[:, 1 : 2 * P : 2]
         x1_low = held.tile([C, P], BF16, name="x1_low")
         nc.gpsimd.tensor_tensor(x1_low[:], rest[:], rest_high, ALU.subtract)
-        yT_ps = [banks.tile([P, C], F32, name=f"yT_ps{t}") for t in range(B)]
+        yT_ps = [banks.tile([P, C], BF16, name=f"yT_ps{t}") for t in range(B)]
         yT = held.tile([P, B, C], BF16, name="yT")
         for t in range(B):
             nc.tensor.matmul(yT_ps[t][:], lhsT=x_bf[:, t * P : (t + 1) * P], rhs=w_bf[:], start=True, stop=True)

import concourse.mybir as mybir
from concourse.masks import make_identity

F32, BF16, U16 = mybir.dt.float32, mybir.dt.bfloat16, mybir.dt.uint16
ALU = mybir.AluOpType
ACT = mybir.ActivationFunctionType
AXIS = mybir.AxisListType

C, S, N, B, P = 128, 512, 256, 2, 128
SLOPE = 0.01
FLOPS = 2 * C * C * N + 2 * C * P * N


def tile_multiheadgraphconvlayer_kernel(tc, base, x, score, mask, w, b, offs, out):
    nc = tc.nc
    with tc.tile_pool(name="held", bufs=1) as held, tc.psum_pool(name="banks", bufs=1) as banks:
        score_sb = held.tile([P, B, P], F32, name="score_sb")
        nc.sync.dma_start(score_sb[:], score.rearrange("t i k -> i t k"))
        x_sb = held.tile([C, N], F32, name="x_sb")
        nc.scalar.dma_start(x_sb[:], x)
        mask_sb = held.tile([P, B, P], F32, name="mask_sb")
        nc.sync.dma_start(mask_sb[:], mask.rearrange("t i k -> i t k"))
        w_sb = held.tile([C, C], F32, name="w_sb")
        nc.scalar.dma_start(w_sb[:], w)
        b_sb = held.tile([C, 1], F32, name="b_sb")
        nc.sync.dma_start(b_sb[:], b)
        offsets = held.tile([128, N // 16], U16, name="offsets")
        nc.sync.dma_start(offsets[:], offs)
        window = held.tile([C, S], F32, name="window")
        nc.sync.dma_start(window[:], base)

        scratch = held.tile([P, 1], F32, name="scratch")
        nc.vector.memset(scratch[:], 0.0)
        nc.scalar.activation(scratch[:], scratch[:], ACT.Exp)

        identity = held.tile([P, P], BF16, name="identity")
        make_identity(nc, identity[:])

        negmax = held.tile([P, B], F32, name="negmax")
        e = held.tile([P, B, P], F32, name="e")
        rowsum = held.tile([P, B], F32, name="rowsum")
        rinv = held.tile([P, B], F32, name="rinv")
        for t in range(B):
            nc.vector.tensor_reduce(negmax[:, t : t + 1], score_sb[:, t, :], axis=AXIS.X, op=ALU.max, negate=True)
            nc.scalar.activation(
                e[:, t, :], score_sb[:, t, :], ACT.Exp, bias=negmax[:, t : t + 1], accum_out=rowsum[:, t : t + 1]
            )
        x_bf = held.tile([C, N], BF16, name="x_bf")
        nc.vector.tensor_copy(x_bf[:], x_sb[:])
        w_bf = held.tile([C, C], BF16, name="w_bf")
        nc.scalar.copy(w_bf[:], w_sb[:])
        x1 = x_sb[:, P:N]
        x1_high = x1.bitcast(BF16)[:, 1 : 2 * P : 2]
        rest = held.tile([C, P], F32, name="rest")
        nc.gpsimd.tensor_tensor(rest[:], x1, x1_high, ALU.subtract)
        rest_high = rest[:].bitcast(BF16)[:, 1 : 2 * P : 2]
        x1_low = held.tile([C, P], BF16, name="x1_low")
        nc.gpsimd.tensor_tensor(x1_low[:], rest[:], rest_high, ALU.subtract)
        yT_ps = [banks.tile([P, C], BF16, name=f"yT_ps{t}") for t in range(B)]
        yT = held.tile([P, B, C], BF16, name="yT")
        for t in range(B):
            nc.tensor.matmul(yT_ps[t][:], lhsT=x_bf[:, t * P : (t + 1) * P], rhs=w_bf[:], start=True, stop=True)
            nc.scalar.copy(yT[:, t, :], yT_ps[t][:])

        att = held.tile([P, B, P], BF16, name="att")
        attT_ps = [banks.tile([P, P], BF16, name=f"attT_ps{t}") for t in range(B)]
        for t in range(B):
            nc.vector.reciprocal(rinv[:, t : t + 1], rowsum[:, t : t + 1])
            nc.vector.scalar_tensor_tensor(
                att[:, t, :], e[:, t, :], rinv[:, t : t + 1], mask_sb[:, t, :], ALU.mult, ALU.mult
            )
            nc.tensor.transpose(attT_ps[t][:], att[:, t, :], identity[:])

        attT = held.tile([P, B, P], BF16, name="attT")
        v_ps = [banks.tile([C, P], F32, name=f"v_ps{t}") for t in range(B)]
        for n, term in enumerate((x1_high, rest_high, x1_low[:])):
            nc.tensor.matmul(v_ps[1][:], lhsT=identity[:], rhs=term, start=n == 0, stop=False)
        for t in range(B):
            nc.vector.tensor_copy(attT[:, t, :], attT_ps[t][:])
            nc.tensor.matmul(v_ps[t][:], lhsT=yT[:, t, :], rhs=attT[:, t, :], start=t == 0, stop=True)

        negb = held.tile([C, 1], F32, name="negb")
        nc.scalar.mul(negb[:], b_sb[:], -1.0)
        v = held.tile([C, N], F32, name="v")
        slope = held.tile([C, N], F32, name="slope")
        nc.vector.scalar_tensor_tensor(v[:, 0:P], v_ps[0][:], b_sb[:, 0:1], x_sb[:, 0:P], ALU.add, ALU.add)
        nc.vector.tensor_scalar(slope[:, P:N], v_ps[1][:], negb[:, 0:1], SLOPE, ALU.is_ge, ALU.max)
        nc.vector.tensor_scalar(v[:, P:N], v_ps[1][:], b_sb[:, 0:1], None, ALU.add)
        nc.vector.tensor_scalar(slope[:, 0:P], v[:, 0:P], 0.0, SLOPE, ALU.is_ge, ALU.max)

        nc.vector.tensor_tensor(window[:].indirect(offsets[:]), v[:], slope[:], ALU.mult)
        nc.sync.dma_start(out, window[:])
